import numpy as np
import ml_dtypes


def mxq(x, axis, fmt="e4m3"):
    dtype, down = {"e4m3": (ml_dtypes.float8_e4m3fn, 7), "e5m2": (ml_dtypes.float8_e5m2, 14)}[fmt]
    v = np.moveaxis(np.asarray(x, np.float32).astype(ml_dtypes.bfloat16).astype(np.float64), axis, -1)
    blocks = v.reshape(v.shape[:-1] + (-1, 32))
    amax = np.abs(blocks).max(-1, keepdims=True)
    byte = np.maximum(np.where(amax > 0, np.frexp(amax)[1] - 1 + 127, 0) - down, 1)
    scale = np.exp2(byte - 127.0)
    codes = (blocks / scale).astype(np.float32).astype(dtype).astype(np.float64)
    return np.moveaxis((codes * scale).reshape(v.shape), -1, axis)


WIDE = False


def mx_kscale(k):
    if not WIDE:
        return np.ones(k)
    levels = np.array([10, -10, 5, -5, 0])
    a = np.random.permutation(np.resize(levels, k // 512 * 4)).reshape(k // 512, 4)
    idx = np.arange(k)
    return np.exp2(a[idx // 512, idx % 128 // 32])


BF16 = ml_dtypes.bfloat16


def bf(x):
    return np.asarray(x, np.float32).astype(BF16)


def f64(x):
    return np.asarray(x).astype(np.float64)


E, T, G, C = 256, 3, 3, 1024


def silu(v):
    return v / (1.0 + np.exp(-v))


def setup_inputs():
    n = np.random.standard_normal
    s = mx_kscale(C)
    t = mx_kscale(G * C).reshape(G, C)
    r = np.sqrt(C)
    return {
        "edge": bf(n((E, C)) * s),
        "edge_nei_len": bf(n((E, T, C)) * s),
        "edge_nei_angle": bf(n((E, T, C)) * s),
        "Wk": bf(n((C, C)) / r / s[:, None] * t[0]),
        "bk": bf(n(C) * 0.2 * t[0]),
        "Wke": bf(n((T, C, C)) / r / s[:, None] * t[1]),
        "bke": bf(n((T, C)) * 0.2 * t[1]),
        "We": bf(n((C, C)) / r / s[:, None] * t[2]),
        "Wk1": bf(n((G * C, C)) / np.sqrt(G * C) / t.reshape(G * C, 1)),
        "bk1": bf(n(C) * 0.2),
    }


def reference(edge, edge_nei_len, edge_nei_angle, Wk, bk, Wke, bke, We, Wk1, bk1):
    kx = (mxq(f64(edge), 1, "e4m3") @ mxq(f64(Wk), 0, "e4m3")) + f64(bk)
    ky = (mxq(f64(edge_nei_len).transpose(1, 0, 2), 2, "e4m3") @ mxq(f64(Wke), 1, "e4m3")) + f64(bke)[:, None, :]
    ky = ky.transpose(1, 0, 2)
    exy = mxq(f64(edge_nei_angle), 2, "e4m3") @ mxq(f64(We), 0, "e4m3")
    w_x, w_y, w_e = f64(Wk1).reshape(G, C, C)
    pre = ((mxq(kx, 1, "e4m3") @ mxq(w_x, 0, "e4m3"))[:, None, :]
           + (mxq(ky, 2, "e4m3") @ mxq(w_y, 0, "e4m3"))
           + (mxq(exy, 2, "e4m3") @ mxq(w_e, 0, "e4m3"))
           + f64(bk1))
    return silu(pre)

@@ -1,0 +1,231 @@
+from contextlib import ExitStack
+
+import concourse.mybir as mybir
+from concourse.masks import make_identity
+
+F32 = mybir.dt.float32
+BF16 = mybir.dt.bfloat16
+U32 = mybir.dt.uint32
+U8 = mybir.dt.uint8
+FP8X4 = mybir.dt.float8_e4m3fn_x4
+ADD = mybir.AluOpType.add
+SILU = mybir.ActivationFunctionType.Silu
+
+P = 128
+PACK = 4
+K_PASS = P * PACK
+BANK = 512
+
+E = 256
+T = 3
+C = 1024
+E_BLOCKS = E // P
+PASSES = C // K_PASS
+STREAMS = 3
+UNITS = 1 + T + T
+HALF = BANK
+
+FLOPS = 2 * 2 * UNITS * E * C * C
+
+
+def tile_comformerconvedgelayer_pa_kernel(
+    tc, edge, edge_nei_len, edge_nei_angle, Wk, bk, Wke, bke, We, Wk1, bk1, out
+):
+    nc = tc.nc
+    with ExitStack() as ctx:
+        consts = ctx.enter_context(tc.tile_pool(name="consts", bufs=1))
+        keep = ctx.enter_context(tc.tile_pool(name="keep", bufs=1))
+        raw_pool = ctx.enter_context(tc.tile_pool(name="raw", bufs=5))
+        grouped_pool = ctx.enter_context(tc.tile_pool(name="grouped", bufs=3))
+        first_w_pool = ctx.enter_context(tc.tile_pool(name="first_w", bufs=2))
+        act_pool = ctx.enter_context(tc.tile_pool(name="act", bufs=2))
+        result_pool = ctx.enter_context(tc.tile_pool(name="result", bufs=4))
+        psum = ctx.enter_context(tc.psum_pool(name="psum", bufs=8))
+
+        warm = consts.tile([P, 1], F32)
+        nc.vector.memset(warm[:], 0.0)
+        nc.scalar.activation(out=warm[:], in_=warm[:], func=SILU)
+
+        ident_f32 = consts.tile([P, P], F32)
+        make_identity(nc, ident_f32[:])
+        ident_bf16 = consts.tile([P, P], BF16)
+        make_identity(nc, ident_bf16[:])
+
+        bias_rows = consts.tile([P, P], BF16)
+        nc.vector.memset(bias_rows[:], 0.0)
+        m_tiles = C // P
+        nc.scalar.dma_start(out=bias_rows[0:m_tiles, :], in_=bk.rearrange("(m p) -> m p", p=P))
+        nc.scalar.dma_start(
+            out=bias_rows[m_tiles : (1 + T) * m_tiles, :],
+            in_=bke.rearrange("t (m p) -> (t m) p", p=P),
+        )
+        bias_cols = psum.tile([P, P], BF16, tag="bank")
+        nc.tensor.transpose(bias_cols[:], bias_rows[:], ident_bf16[:])
+        first_bias = consts.tile([P, (1 + T) * m_tiles], F32)
+        nc.vector.tensor_copy(out=first_bias[:], in_=bias_cols[:, 0 : (1 + T) * m_tiles])
+
+        bk1_row = consts.tile([P, C], BF16)
+        nc.vector.memset(bk1_row[:], 0.0)
+        nc.scalar.dma_start(out=bk1_row[0:1, :], in_=bk1.rearrange("(o c) -> o c", o=1))
+        ones = consts.tile([P, P], BF16)
+        nc.vector.memset(ones[:], 1.0)
+        bk1_all = consts.tile([P, C], F32)
+        for h in range(C // BANK):
+            cols = slice(h * BANK, (h + 1) * BANK)
+            spread = psum.tile([P, BANK], F32, tag="bank")
+            nc.tensor.matmul(out=spread[:], lhsT=ones[:], rhs=bk1_row[:, cols], start=True, stop=True)
+            nc.vector.tensor_copy(out=bk1_all[:, cols], in_=spread[:])
+
+        x_words = keep.tile([P, UNITS, PASSES * E], U32, align_bytes=64)
+        x_scales = keep.tile([P, UNITS, PASSES * E], U8, align_bytes=64)
+        h_words = keep.tile([P, UNITS, PASSES * E], U32, align_bytes=64)
+        h_scales = keep.tile([P, UNITS, PASSES * E], U8, align_bytes=64)
+        n_halves = C // BANK
+        w2_words = keep.tile([P, n_halves, STREAMS * PASSES, BANK], U32, align_bytes=64)
+        w2_scales = keep.tile([P, n_halves, STREAMS * PASSES, BANK], U8, align_bytes=64)
+
+        def regroup_and_quantise(four_rows, words, scales):
+            grouped = grouped_pool.tile([P, 2, HALF, PACK], BF16, align_bytes=64)
+            copies = (nc.vector.tensor_copy, nc.scalar.copy)
+            for half in range(2):
+                copies[half](
+                    out=grouped[:, half].rearrange("p (c i) t -> p c t i", i=4),
+                    in_=four_rows[half].rearrange("p t (c i) -> p c t i", i=4),
+                )
+            for half in range(2):
+                nc.vector.quantize_mx(
+                    out=words[half].bitcast(FP8X4),
+                    scales=scales[half],
+                    in_=grouped[:, half].rearrange("p c t -> p (c t)"),
+                )
+
+        def quantise_activations(unit, rows_of_block):
+            grouped = act_pool.tile([P, PASSES * E * PACK], BF16, align_bytes=64, tag="x_grouped")
+            grouped_pairs = grouped[:].bitcast(F32).rearrange("p (g r u) -> p g r u", g=PASSES, u=2)
+            for b in range(E_BLOCKS):
+                pairs = rows_of_block[b].bitcast(F32)
+                turned = psum.tile([P, BANK], F32, tag="bank")
+                for w in range(BANK // P):
+                    nc.tensor.transpose(
+                        turned[:, w * P : (w + 1) * P], pairs[:, w * P : (w + 1) * P], ident_f32[:]
+                    )
+                nc.scalar.copy(
+                    out=grouped_pairs[:, :, b * P : (b + 1) * P, :],
+                    in_=turned[:].rearrange("p (g u r) -> p g r u", g=PASSES, u=2),
+                )
+            nc.vector.quantize_mx(
+                out=x_words[:, unit, :].bitcast(FP8X4), scales=x_scales[:, unit, :], in_=grouped[:]
+            )
+
+        def load_first_weight(w):
+            words = first_w_pool.tile([P, PASSES, C], U32, align_bytes=64, tag="w1_words")
+            scales = first_w_pool.tile([P, PASSES, C], U8, align_bytes=64, tag="w1_scales")
+            for g in range(PASSES):
+                raw = raw_pool.tile([P, PACK, C], BF16, tag="raw")
+                nc.sync.dma_start(
+                    out=raw[:].rearrange("p (u e) c -> p u (e c)", u=2),
+                    in_=w[g * K_PASS : (g + 1) * K_PASS, :].rearrange("(u p e) c -> p u (e c)", u=2, e=2),
+                )
+                halves = [slice(half * HALF, (half + 1) * HALF) for half in range(2)]
+                regroup_and_quantise(
+                    [raw[:, :, cols] for cols in halves],
+                    [words[:, g, cols] for cols in halves],
+                    [scales[:, g, cols] for cols in halves],
+                )
+            return words, scales
+
+        def first_product(unit, words, scales, bias_row):
+            grouped = act_pool.tile([P, PASSES * E_BLOCKS, P, PACK], BF16, align_bytes=64, tag="h_grouped")
+            for q in range(PASSES):
+                for b in range(E_BLOCKS):
+                    acc = psum.tile([P, BANK], F32, tag="bank")
+                    for j in range(PACK):
+                        m_cols = slice((q * PACK + j) * P, (q * PACK + j + 1) * P)
+                        for g in range(PASSES):
+                            e_cols = slice(g * E + b * P, g * E + (b + 1) * P)
+                            nc.tensor.matmul_mx(
+                                out=acc[:, j * P : (j + 1) * P],
+                                lhsT=words[:, g, m_cols].bitcast(FP8X4),
+                                lhsT_scale=scales[:, g, m_cols],
+                                rhs=x_words[:, unit, e_cols].bitcast(FP8X4),
+                                rhs_scale=x_scales[:, unit, e_cols],
+                                start=(g == 0),
+                                stop=(g == PASSES - 1),
+                            )
+                    interleaved = acc[:].rearrange("p (j r) -> p r j", j=PACK)
+                    if bias_row is None:
+                        nc.scalar.copy(out=grouped[:, q * E_BLOCKS + b], in_=interleaved)
+                    else:
+                        first = bias_row * m_tiles + q * PACK
+                        nc.vector.tensor_tensor(
+                            out=grouped[:, q * E_BLOCKS + b],
+                            in0=interleaved,
+                            in1=first_bias[:, first : first + PACK].unsqueeze(1).to_broadcast([P, P, PACK]),
+                            op=ADD,
+                        )
+            nc.vector.quantize_mx(
+                out=h_words[:, unit, :].bitcast(FP8X4),
+                scales=h_scales[:, unit, :],
+                in_=grouped[:].rearrange("p a r j -> p (a r j)"),
+            )
+
+        edge_sb = keep.tile([P, E_BLOCKS, C], BF16)
+        nc.sync.dma_start(out=edge_sb[:], in_=edge.rearrange("(b p) k -> p b k", p=P))
+        quantise_activations(0, [edge_sb[:, b, :] for b in range(E_BLOCKS)])
+        words, scales = load_first_weight(Wk)
+        first_product(0, words, scales, 0)
+
+        len_sb = keep.tile([P, E_BLOCKS, T, C], BF16)
+        for b in range(E_BLOCKS):
+            nc.sync.dma_start(out=len_sb[:, b], in_=edge_nei_len[b * P : (b + 1) * P])
+        for t in range(T):
+            quantise_activations(1 + t, [len_sb[:, b, t, :] for b in range(E_BLOCKS)])
+        for t in range(T):
+            words, scales = load_first_weight(Wke[t])
+            first_product(1 + t, words, scales, 1 + t)
+
+        angle_sb = keep.tile([P, E_BLOCKS, T, C], BF16)
+        for b in range(E_BLOCKS):
+            nc.sync.dma_start(out=angle_sb[:, b], in_=edge_nei_angle[b * P : (b + 1) * P])
+        for t in range(T):
+            quantise_activations(1 + T + t, [angle_sb[:, b, t, :] for b in range(E_BLOCKS)])
+        words, scales = load_first_weight(We)
+        for t in range(T):
+            first_product(1 + T + t, words, scales, None)
+
+        for h in range(n_halves):
+            n_cols = slice(h * BANK, (h + 1) * BANK)
+            accs = [psum.tile([P, BANK], F32, tag="bank", name="acc2") for i in range(E_BLOCKS * T)]
+            for s in range(STREAMS):
+                raw = raw_pool.tile([P, PASSES, PACK, BANK], BF16, tag="raw")
+                nc.sync.dma_start(
+                    out=raw[:].rearrange("p q j n -> p (q j) n"),
+                    in_=Wk1[s * C : (s + 1) * C, n_cols].rearrange("(a p) n -> p a n", p=P),
+                )
+                regroup_and_quantise(
+                    [raw[:, q] for q in range(PASSES)],
+                    [w2_words[:, h, s * PASSES + q, :] for q in range(PASSES)],
+                    [w2_scales[:, h, s * PASSES + q, :] for q in range(PASSES)],
+                )
+                for q in range(PASSES):
+                    for b in range(E_BLOCKS):
+                        for t in range(T):
+                            unit = 0 if s == 0 else 1 + (s - 1) * T + t
+                            e_cols = slice((q * E_BLOCKS + b) * P, (q * E_BLOCKS + b + 1) * P)
+                            nc.tensor.matmul_mx(
+                                out=accs[b * T + t][:],
+                                lhsT=h_words[:, unit, e_cols].bitcast(FP8X4),
+                                lhsT_scale=h_scales[:, unit, e_cols],
+                                rhs=w2_words[:, h, s * PASSES + q, :].bitcast(FP8X4),
+                                rhs_scale=w2_scales[:, h, s * PASSES + q, :],
+                                start=(s == 0 and q == 0),
+                                stop=(s == STREAMS - 1 and q == PASSES - 1),
+                            )
+            for b in range(E_BLOCKS):
+                for t in range(T):
+                    result = result_pool.tile([P, BANK], F32)
+                    nc.vector.tensor_tensor(
+                        out=result[:], in0=accs[b * T + t][:], in1=bk1_all[:, n_cols], op=ADD
+                    )
+                    nc.scalar.activation(out=result[:], in_=result[:], func=SILU)
+                    nc.scalar.dma_start(out=out[b * P : (b + 1) * P, t, n_cols], in_=result[:])

@@ -24,6 +24,10 @@ PASSES = C // K_PASS
 STREAMS = 3
 UNITS = 1 + T + T
 HALF = BANK
+FIRST_WEIGHTS = 2 + T
+FIRST_CHUNKS = FIRST_WEIGHTS * PASSES
+SECOND_ORDER = (0, 2, 1)
+RAW_BUFS = 4
 
 FLOPS = 2 * 2 * UNITS * E * C * C
 
@@ -32,15 +36,31 @@ def tile_comformerconvedgelayer_pa_kernel(
     tc, edge, edge_nei_len, edge_nei_angle, Wk, bk, Wke, bke, We, Wk1, bk1, out
 ):
     nc = tc.nc
+    m_tiles = C // P
+    n_halves = C // BANK
     with ExitStack() as ctx:
         consts = ctx.enter_context(tc.tile_pool(name="consts", bufs=1))
         keep = ctx.enter_context(tc.tile_pool(name="keep", bufs=1))
-        raw_pool = ctx.enter_context(tc.tile_pool(name="raw", bufs=5))
+        raw_pool = ctx.enter_context(tc.tile_pool(name="raw", bufs=RAW_BUFS))
         grouped_pool = ctx.enter_context(tc.tile_pool(name="grouped", bufs=3))
         first_w_pool = ctx.enter_context(tc.tile_pool(name="first_w", bufs=2))
-        act_pool = ctx.enter_context(tc.tile_pool(name="act", bufs=2))
-        result_pool = ctx.enter_context(tc.tile_pool(name="result", bufs=4))
+        act_pool = ctx.enter_context(tc.tile_pool(name="act", bufs=4))
+        result_pool = ctx.enter_context(tc.tile_pool(name="result", bufs=E_BLOCKS * T))
         psum = ctx.enter_context(tc.psum_pool(name="psum", bufs=8))
+        ctx.enter_context(tc.manual_schedule())
+
+        bias_rows = consts.tile([P, P], BF16)
+        nc.vector.memset(bias_rows[:], 0.0)
+        nc.scalar.dma_start(out=bias_rows[0:m_tiles, :], in_=bk.rearrange("(m p) -> m p", p=P))
+        nc.scalar.dma_start(
+            out=bias_rows[m_tiles : (1 + T) * m_tiles, :],
+            in_=bke.rearrange("t (m p) -> (t m) p", p=P),
+        )
+        bk1_row = consts.tile([P, C], BF16)
+        nc.vector.memset(bk1_row[:], 0.0)
+        nc.scalar.dma_start(out=bk1_row[0:1, :], in_=bk1.rearrange("(o c) -> o c", o=1))
+        ones = consts.tile([P, P], BF16)
+        nc.vector.memset(ones[:], 1.0)
 
         warm = consts.tile([P, 1], F32)
         nc.vector.memset(warm[:], 0.0)
@@ -50,60 +70,96 @@ def tile_comformerconvedgelayer_pa_kernel(
         make_identity(nc, ident_f32[:])
         ident_bf16 = consts.tile([P, P], BF16)
         make_identity(nc, ident_bf16[:])
-
-        bias_rows = consts.tile([P, P], BF16)
-        nc.vector.memset(bias_rows[:], 0.0)
-        m_tiles = C // P
-        nc.scalar.dma_start(out=bias_rows[0:m_tiles, :], in_=bk.rearrange("(m p) -> m p", p=P))
-        nc.scalar.dma_start(
-            out=bias_rows[m_tiles : (1 + T) * m_tiles, :],
-            in_=bke.rearrange("t (m p) -> (t m) p", p=P),
-        )
-        bias_cols = psum.tile([P, P], BF16, tag="bank")
-        nc.tensor.transpose(bias_cols[:], bias_rows[:], ident_bf16[:])
         first_bias = consts.tile([P, (1 + T) * m_tiles], F32)
-        nc.vector.tensor_copy(out=first_bias[:], in_=bias_cols[:, 0 : (1 + T) * m_tiles])
-
-        bk1_row = consts.tile([P, C], BF16)
-        nc.vector.memset(bk1_row[:], 0.0)
-        nc.scalar.dma_start(out=bk1_row[0:1, :], in_=bk1.rearrange("(o c) -> o c", o=1))
-        ones = consts.tile([P, P], BF16)
-        nc.vector.memset(ones[:], 1.0)
         bk1_all = consts.tile([P, C], F32)
-        for h in range(C // BANK):
-            cols = slice(h * BANK, (h + 1) * BANK)
-            spread = psum.tile([P, BANK], F32, tag="bank")
-            nc.tensor.matmul(out=spread[:], lhsT=ones[:], rhs=bk1_row[:, cols], start=True, stop=True)
-            nc.vector.tensor_copy(out=bk1_all[:, cols], in_=spread[:])
 
         x_words = keep.tile([P, UNITS, PASSES * E], U32, align_bytes=64)
         x_scales = keep.tile([P, UNITS, PASSES * E], U8, align_bytes=64)
         h_words = keep.tile([P, UNITS, PASSES * E], U32, align_bytes=64)
         h_scales = keep.tile([P, UNITS, PASSES * E], U8, align_bytes=64)
-        n_halves = C // BANK
         w2_words = keep.tile([P, n_halves, STREAMS * PASSES, BANK], U32, align_bytes=64)
         w2_scales = keep.tile([P, n_halves, STREAMS * PASSES, BANK], U8, align_bytes=64)
+        we_words = keep.tile([P, PASSES, C], U32, align_bytes=64)
+        we_scales = keep.tile([P, PASSES, C], U8, align_bytes=64)
+        w1_words = {0: we_words}
+        w1_scales = {0: we_scales}
 
-        def regroup_and_quantise(four_rows, words, scales):
-            grouped = grouped_pool.tile([P, 2, HALF, PACK], BF16, align_bytes=64)
-            copies = (nc.vector.tensor_copy, nc.scalar.copy)
-            for half in range(2):
-                copies[half](
-                    out=grouped[:, half].rearrange("p (c i) t -> p c t i", i=4),
-                    in_=four_rows[half].rearrange("p t (c i) -> p c t i", i=4),
+        chunk_sources = []
+        for w in (We, Wk, Wke[0], Wke[1], Wke[2]):
+            for g in range(PASSES):
+                chunk_sources.append(
+                    w[g * K_PASS : (g + 1) * K_PASS, :].rearrange("(u p e) c -> p u (e c)", u=2, e=2)
                 )
+        for h in range(n_halves):
+            for s in SECOND_ORDER:
+                chunk_sources.append(
+                    Wk1[s * C : (s + 1) * C, h * BANK : (h + 1) * BANK].rearrange("(a p) n -> p a n", p=P)
+                )
+        chunks = []
+        regrouped = {}
+
+        def load_next_chunk():
+            index = len(chunks)
+            if index == len(chunk_sources):
+                return
+            if index < FIRST_CHUNKS:
+                raw = raw_pool.tile([P, PACK, C], BF16, tag="raw")
+                nc.sync.dma_start(
+                    out=raw[:].rearrange("p (u e) c -> p u (e c)", u=2), in_=chunk_sources[index]
+                )
+                chunks.append([raw[:, :, half * HALF : (half + 1) * HALF] for half in range(2)])
+            else:
+                raw = raw_pool.tile([P, PASSES * PACK, BANK], BF16, tag="raw")
+                nc.sync.dma_start(out=raw[:], in_=chunk_sources[index])
+                chunks.append([raw[:, q * PACK : (q + 1) * PACK, :] for q in range(PASSES)])
+
+        def regroup(index):
+            by_vector = grouped_pool.tile([P, HALF, PACK], BF16, align_bytes=64, bufs=2)
+            by_scalar = grouped_pool.tile([P, HALF, PACK], BF16, align_bytes=64)
+            nc.vector.tensor_copy(
+                out=by_vector[:].rearrange("p (c i) t -> p c t i", i=4),
+                in_=chunks[index][0].rearrange("p t (c i) -> p c t i", i=4),
+            )
+            nc.scalar.copy(
+                out=by_scalar[:].rearrange("p (c i) t -> p c t i", i=4),
+                in_=chunks[index][1].rearrange("p t (c i) -> p c t i", i=4),
+            )
+            regrouped[index] = (by_vector, by_scalar)
+            load_next_chunk()
+
+        def quantise_chunk(index):
             for half in range(2):
+                if index < FIRST_CHUNKS:
+                    weight, g = divmod(index, PASSES)
+                    cols = slice(half * HALF, (half + 1) * HALF)
+                    words, scales = w1_words[weight][:, g, cols], w1_scales[weight][:, g, cols]
+                else:
+                    h, position = divmod(index - FIRST_CHUNKS, STREAMS)
+                    q = SECOND_ORDER[position] * PASSES + half
+                    words, scales = w2_words[:, h, q, :], w2_scales[:, h, q, :]
                 nc.vector.quantize_mx(
-                    out=words[half].bitcast(FP8X4),
-                    scales=scales[half],
-                    in_=grouped[:, half].rearrange("p c t -> p (c t)"),
+                    out=words.bitcast(FP8X4),
+                    scales=scales,
+                    in_=regrouped[index][half][:].rearrange("p c t -> p (c t)"),
                 )
 
-        def quantise_activations(unit, rows_of_block):
+        angle_sb = keep.tile([P, E_BLOCKS, T, C], BF16)
+        edge_sb = keep.tile([P, E_BLOCKS, C], BF16)
+        len_sb = keep.tile([P, E_BLOCKS, T, C], BF16)
+        x_grouped = {}
+
+        def rows_of(unit, b):
+            if unit == 0:
+                return edge_sb[:, b, :]
+            if unit <= T:
+                return len_sb[:, b, unit - 1, :]
+            return angle_sb[:, b, unit - 1 - T, :]
+
+        def transpose_activations(unit):
             grouped = act_pool.tile([P, PASSES * E * PACK], BF16, align_bytes=64, tag="x_grouped")
             grouped_pairs = grouped[:].bitcast(F32).rearrange("p (g r u) -> p g r u", g=PASSES, u=2)
             for b in range(E_BLOCKS):
-                pairs = rows_of_block[b].bitcast(F32)
+                pairs = rows_of(unit, b).bitcast(F32)
                 turned = psum.tile([P, BANK], F32, tag="bank")
                 for w in range(BANK // P):
                     nc.tensor.transpose(
@@ -113,29 +169,22 @@ def tile_comformerconvedgelayer_pa_kernel(
                     out=grouped_pairs[:, :, b * P : (b + 1) * P, :],
                     in_=turned[:].rearrange("p (g u r) -> p g r u", g=PASSES, u=2),
                 )
+            x_grouped[unit] = grouped
+
+        def quantise_activations(unit):
             nc.vector.quantize_mx(
-                out=x_words[:, unit, :].bitcast(FP8X4), scales=x_scales[:, unit, :], in_=grouped[:]
+                out=x_words[:, unit, :].bitcast(FP8X4),
+                scales=x_scales[:, unit, :],
+                in_=x_grouped[unit][:],
             )
 
-        def load_first_weight(w):
-            words = first_w_pool.tile([P, PASSES, C], U32, align_bytes=64, tag="w1_words")
-            scales = first_w_pool.tile([P, PASSES, C], U8, align_bytes=64, tag="w1_scales")
-            for g in range(PASSES):
-                raw = raw_pool.tile([P, PACK, C], BF16, tag="raw")
-                nc.sync.dma_start(
-                    out=raw[:].rearrange("p (u e) c -> p u (e c)", u=2),
-                    in_=w[g * K_PASS : (g + 1) * K_PASS, :].rearrange("(u p e) c -> p u (e c)", u=2, e=2),
-                )
-                halves = [slice(half * HALF, (half + 1) * HALF) for half in range(2)]
-                regroup_and_quantise(
-                    [raw[:, :, cols] for cols in halves],
-                    [words[:, g, cols] for cols in halves],
-                    [scales[:, g, cols] for cols in halves],
-                )
-            return words, scales
+        first_accs = {}
+        h_grouped = {}
 
-        def first_product(unit, words, scales, bias_row):
-            grouped = act_pool.tile([P, PASSES * E_BLOCKS, P, PACK], BF16, align_bytes=64, tag="h_grouped")
+        def first_passes(unit):
+            weight = 1 + unit if unit <= T else 0
+            words, scales = w1_words[weight], w1_scales[weight]
+            first_accs[unit] = []
             for q in range(PASSES):
                 for b in range(E_BLOCKS):
                     acc = psum.tile([P, BANK], F32, tag="bank")
@@ -152,75 +201,54 @@ def tile_comformerconvedgelayer_pa_kernel(
                                 start=(g == 0),
                                 stop=(g == PASSES - 1),
                             )
-                    interleaved = acc[:].rearrange("p (j r) -> p r j", j=PACK)
-                    if bias_row is None:
-                        nc.scalar.copy(out=grouped[:, q * E_BLOCKS + b], in_=interleaved)
-                    else:
-                        first = bias_row * m_tiles + q * PACK
-                        nc.vector.tensor_tensor(
-                            out=grouped[:, q * E_BLOCKS + b],
-                            in0=interleaved,
-                            in1=first_bias[:, first : first + PACK].unsqueeze(1).to_broadcast([P, P, PACK]),
-                            op=ADD,
-                        )
+                    first_accs[unit].append(acc)
+
+        def first_out(unit):
+            grouped = act_pool.tile([P, PASSES * E_BLOCKS, P, PACK], BF16, align_bytes=64, tag="h_grouped", bufs=3)
+            for a, acc in enumerate(first_accs[unit]):
+                interleaved = acc[:].rearrange("p (j r) -> p r j", j=PACK)
+                if unit > T:
+                    nc.scalar.copy(out=grouped[:, a], in_=interleaved)
+                else:
+                    first = unit * m_tiles + (a // E_BLOCKS) * PACK
+                    nc.vector.tensor_tensor(
+                        out=grouped[:, a],
+                        in0=interleaved,
+                        in1=first_bias[:, first : first + PACK].unsqueeze(1).to_broadcast([P, P, PACK]),
+                        op=ADD,
+                    )
+            h_grouped[unit] = grouped
+
+        def quantise_hidden(unit):
             nc.vector.quantize_mx(
                 out=h_words[:, unit, :].bitcast(FP8X4),
                 scales=h_scales[:, unit, :],
-                in_=grouped[:].rearrange("p a r j -> p (a r j)"),
+                in_=h_grouped[unit][:].rearrange("p a r j -> p (a r j)"),
             )
 
-        edge_sb = keep.tile([P, E_BLOCKS, C], BF16)
-        nc.sync.dma_start(out=edge_sb[:], in_=edge.rearrange("(b p) k -> p b k", p=P))
-        quantise_activations(0, [edge_sb[:, b, :] for b in range(E_BLOCKS)])
-        words, scales = load_first_weight(Wk)
-        first_product(0, words, scales, 0)
+        def second_passes(index, accs):
+            h, position = divmod(index - FIRST_CHUNKS, STREAMS)
+            s = SECOND_ORDER[position]
+            for q in range(PASSES):
+                for b in range(E_BLOCKS):
+                    for t in range(T):
+                        unit = 0 if s == 0 else 1 + (s - 1) * T + t
+                        e_cols = slice((q * E_BLOCKS + b) * P, (q * E_BLOCKS + b + 1) * P)
+                        nc.tensor.matmul_mx(
+                            out=accs[b * T + t][:],
+                            lhsT=h_words[:, unit, e_cols].bitcast(FP8X4),
+                            lhsT_scale=h_scales[:, unit, e_cols],
+                            rhs=w2_words[:, h, s * PASSES + q, :].bitcast(FP8X4),
+                            rhs_scale=w2_scales[:, h, s * PASSES + q, :],
+                            start=(position == 0 and q == 0),
+                            stop=(position == STREAMS - 1 and q == PASSES - 1),
+                        )
 
-        len_sb = keep.tile([P, E_BLOCKS, T, C], BF16)
-        for b in range(E_BLOCKS):
-            nc.sync.dma_start(out=len_sb[:, b], in_=edge_nei_len[b * P : (b + 1) * P])
-        for t in range(T):
-            quantise_activations(1 + t, [len_sb[:, b, t, :] for b in range(E_BLOCKS)])
-        for t in range(T):
-            words, scales = load_first_weight(Wke[t])
-            first_product(1 + t, words, scales, 1 + t)
+        def open_banks():
+            return [psum.tile([P, BANK], F32, tag="bank", name="acc2") for i in range(E_BLOCKS * T)]
 
-        angle_sb = keep.tile([P, E_BLOCKS, T, C], BF16)
-        for b in range(E_BLOCKS):
-            nc.sync.dma_start(out=angle_sb[:, b], in_=edge_nei_angle[b * P : (b + 1) * P])
-        for t in range(T):
-            quantise_activations(1 + T + t, [angle_sb[:, b, t, :] for b in range(E_BLOCKS)])
-        words, scales = load_first_weight(We)
-        for t in range(T):
-            first_product(1 + T + t, words, scales, None)
-
-        for h in range(n_halves):
+        def finish(h, accs):
             n_cols = slice(h * BANK, (h + 1) * BANK)
-            accs = [psum.tile([P, BANK], F32, tag="bank", name="acc2") for i in range(E_BLOCKS * T)]
-            for s in range(STREAMS):
-                raw = raw_pool.tile([P, PASSES, PACK, BANK], BF16, tag="raw")
-                nc.sync.dma_start(
-                    out=raw[:].rearrange("p q j n -> p (q j) n"),
-                    in_=Wk1[s * C : (s + 1) * C, n_cols].rearrange("(a p) n -> p a n", p=P),
-                )
-                regroup_and_quantise(
-                    [raw[:, q] for q in range(PASSES)],
-                    [w2_words[:, h, s * PASSES + q, :] for q in range(PASSES)],
-                    [w2_scales[:, h, s * PASSES + q, :] for q in range(PASSES)],
-                )
-                for q in range(PASSES):
-                    for b in range(E_BLOCKS):
-                        for t in range(T):
-                            unit = 0 if s == 0 else 1 + (s - 1) * T + t
-                            e_cols = slice((q * E_BLOCKS + b) * P, (q * E_BLOCKS + b + 1) * P)
-                            nc.tensor.matmul_mx(
-                                out=accs[b * T + t][:],
-                                lhsT=h_words[:, unit, e_cols].bitcast(FP8X4),
-                                lhsT_scale=h_scales[:, unit, e_cols],
-                                rhs=w2_words[:, h, s * PASSES + q, :].bitcast(FP8X4),
-                                rhs_scale=w2_scales[:, h, s * PASSES + q, :],
-                                start=(s == 0 and q == 0),
-                                stop=(s == STREAMS - 1 and q == PASSES - 1),
-                            )
             for b in range(E_BLOCKS):
                 for t in range(T):
                     result = result_pool.tile([P, BANK], F32)
@@ -229,3 +257,70 @@ def tile_comformerconvedgelayer_pa_kernel(
                     )
                     nc.scalar.activation(out=result[:], in_=result[:], func=SILU)
                     nc.scalar.dma_start(out=out[b * P : (b + 1) * P, t, n_cols], in_=result[:])
+
+        load_next_chunk()
+        load_next_chunk()
+        for b in range(E_BLOCKS):
+            nc.sync.dma_start(out=angle_sb[:, b], in_=edge_nei_angle[b * P : (b + 1) * P])
+        load_next_chunk()
+        nc.sync.dma_start(out=edge_sb[:], in_=edge.rearrange("(b p) k -> p b k", p=P))
+
+        for phase in range(FIRST_WEIGHTS + 1):
+            arriving = phase - 1
+            complete = phase - 2
+            exy_out = T + phase - 1
+            if 1 <= phase < FIRST_WEIGHTS:
+                w1_words[phase] = first_w_pool.tile([P, PASSES, C], U32, align_bytes=64, name="w1_words")
+                w1_scales[phase] = first_w_pool.tile([P, PASSES, C], U8, align_bytes=64, name="w1_scales")
+
+            regroup(2 * phase)
+            if phase == 0:
+                for b in range(E_BLOCKS):
+                    nc.sync.dma_start(out=len_sb[:, b], in_=edge_nei_len[b * P : (b + 1) * P])
+            if phase > 0:
+                quantise_chunk(2 * phase - 1)
+            if phase == 1:
+                for t in range(T):
+                    transpose_activations(1 + T + t)
+                bias_cols = psum.tile([P, P], BF16, tag="bank")
+                nc.tensor.transpose(bias_cols[:], bias_rows[:], ident_bf16[:])
+                nc.vector.tensor_copy(out=first_bias[:], in_=bias_cols[:, 0 : (1 + T) * m_tiles])
+            if 0 <= arriving <= T:
+                transpose_activations(arriving)
+            if complete >= 0:
+                first_passes(complete)
+            if 2 <= phase <= 1 + T:
+                first_out(exy_out)
+
+            regroup(2 * phase + 1)
+            quantise_chunk(2 * phase)
+            if phase == 1:
+                for t in range(T):
+                    quantise_activations(1 + T + t)
+            if 0 <= arriving <= T:
+                quantise_activations(arriving)
+            if complete >= 0:
+                first_out(complete)
+                quantise_hidden(complete)
+            if 2 <= phase <= 1 + T:
+                quantise_hidden(exy_out)
+            if 1 <= phase <= T:
+                first_passes(T + phase)
+
+        for h in range(n_halves):
+            cols = slice(h * BANK, (h + 1) * BANK)
+            spread = psum.tile([P, BANK], F32, tag="bank")
+            nc.tensor.matmul(out=spread[:], lhsT=ones[:], rhs=bk1_row[:, cols], start=True, stop=True)
+            nc.vector.tensor_copy(out=bk1_all[:, cols], in_=spread[:])
+
+        accs = open_banks()
+        second_passes(FIRST_CHUNKS, accs)
+        for index in range(FIRST_CHUNKS + 2, len(chunk_sources) + 1):
+            if index < len(chunk_sources):
+                regroup(index)
+            quantise_chunk(index - 1)
+            if index - 1 == FIRST_CHUNKS + STREAMS:
+                finish(0, accs)
+                accs = open_banks()
+            second_passes(index - 1, accs)
+        finish(1, accs)

@@ -47,7 +47,6 @@ def tile_comformerconvedgelayer_pa_kernel(
         act_pool = ctx.enter_context(tc.tile_pool(name="act", bufs=4))
         result_pool = ctx.enter_context(tc.tile_pool(name="result", bufs=E_BLOCKS * T))
         psum = ctx.enter_context(tc.psum_pool(name="psum", bufs=8))
-        ctx.enter_context(tc.manual_schedule())
 
         bias_rows = consts.tile([P, P], BF16)
         nc.vector.memset(bias_rows[:], 0.0)
@@ -143,23 +142,24 @@ def tile_comformerconvedgelayer_pa_kernel(
                     in_=regrouped[index][half][:].rearrange("p c t -> p (c t)"),
                 )
 
-        angle_sb = keep.tile([P, E_BLOCKS, T, C], BF16)
-        edge_sb = keep.tile([P, E_BLOCKS, C], BF16)
-        len_sb = keep.tile([P, E_BLOCKS, T, C], BF16)
+        x_rows = {}
         x_grouped = {}
 
-        def rows_of(unit, b):
+        def load_activations(unit):
             if unit == 0:
-                return edge_sb[:, b, :]
-            if unit <= T:
-                return len_sb[:, b, unit - 1, :]
-            return angle_sb[:, b, unit - 1 - T, :]
+                source = edge
+            elif unit <= T:
+                source = edge_nei_len[:, unit - 1, :]
+            else:
+                source = edge_nei_angle[:, unit - 1 - T, :]
+            x_rows[unit] = keep.tile([P, E_BLOCKS, C], BF16, name="x_rows%d" % unit)
+            nc.sync.dma_start(out=x_rows[unit][:], in_=source.rearrange("(b p) k -> p b k", p=P))
 
         def transpose_activations(unit):
             grouped = act_pool.tile([P, PASSES * E * PACK], BF16, align_bytes=64, tag="x_grouped")
             grouped_pairs = grouped[:].bitcast(F32).rearrange("p (g r u) -> p g r u", g=PASSES, u=2)
             for b in range(E_BLOCKS):
-                pairs = rows_of(unit, b).bitcast(F32)
+                pairs = x_rows[unit][:, b, :].bitcast(F32)
                 turned = psum.tile([P, BANK], F32, tag="bank")
                 for w in range(BANK // P):
                     nc.tensor.transpose(
@@ -260,10 +260,10 @@ def tile_comformerconvedgelayer_pa_kernel(
 
         load_next_chunk()
         load_next_chunk()
-        for b in range(E_BLOCKS):
-            nc.sync.dma_start(out=angle_sb[:, b], in_=edge_nei_angle[b * P : (b + 1) * P])
+        for t in range(T):
+            load_activations(1 + T + t)
+        load_activations(0)
         load_next_chunk()
-        nc.sync.dma_start(out=edge_sb[:], in_=edge.rearrange("(b p) k -> p b k", p=P))
 
         for phase in range(FIRST_WEIGHTS + 1):
             arriving = phase - 1
@@ -274,9 +274,8 @@ def tile_comformerconvedgelayer_pa_kernel(
                 w1_scales[phase] = first_w_pool.tile([P, PASSES, C], U8, align_bytes=64, name="w1_scales")
 
             regroup(2 * phase)
-            if phase == 0:
-                for b in range(E_BLOCKS):
-                    nc.sync.dma_start(out=len_sb[:, b], in_=edge_nei_len[b * P : (b + 1) * P])
+            if phase < T:
+                load_activations(1 + phase)
             if phase > 0:
                 quantise_chunk(2 * phase - 1)
             if phase == 1:

@@ -24,6 +24,7 @@ PASSES = C // K_PASS
 STREAMS = 3
 UNITS = 1 + T + T
 HALF = BANK
+VECTOR_COLS = 448
 FIRST_WEIGHTS = 2 + T
 FIRST_CHUNKS = FIRST_WEIGHTS * PASSES
 SECOND_ORDER = (0, 2, 1)
@@ -83,54 +84,51 @@ def tile_comformerconvedgelayer_pa_kernel(
         w1_words = {0: we_words}
         w1_scales = {0: we_scales}
 
-        chunk_sources = []
-        for w in (We, Wk, Wke[0], Wke[1], Wke[2]):
-            for g in range(PASSES):
-                chunk_sources.append(
-                    w[g * K_PASS : (g + 1) * K_PASS, :].rearrange("(u p e) c -> p u (e c)", u=2, e=2)
-                )
-        for h in range(n_halves):
-            for s in SECOND_ORDER:
-                chunk_sources.append(
-                    Wk1[s * C : (s + 1) * C, h * BANK : (h + 1) * BANK].rearrange("(a p) n -> p a n", p=P)
-                )
         chunks = []
         regrouped = {}
+        first_weights = (We, Wk, Wke[0], Wke[1], Wke[2])
+        n_chunks = FIRST_CHUNKS + n_halves * STREAMS
 
         def load_next_chunk():
             index = len(chunks)
-            if index == len(chunk_sources):
+            if index == n_chunks:
                 return
+            raw = raw_pool.tile([P, PACK, C], BF16)
             if index < FIRST_CHUNKS:
-                raw = raw_pool.tile([P, PACK, C], BF16, tag="raw")
+                weight, g = divmod(index, PASSES)
+                rows = first_weights[weight][g * K_PASS : (g + 1) * K_PASS, :]
                 nc.sync.dma_start(
-                    out=raw[:].rearrange("p (u e) c -> p u (e c)", u=2), in_=chunk_sources[index]
+                    out=raw[:].rearrange("p (u e) c -> p u (e c)", u=2),
+                    in_=rows.rearrange("(u p e) c -> p u (e c)", u=2, e=2),
                 )
-                chunks.append([raw[:, :, half * HALF : (half + 1) * HALF] for half in range(2)])
             else:
-                raw = raw_pool.tile([P, PASSES * PACK, BANK], BF16, tag="raw")
-                nc.sync.dma_start(out=raw[:], in_=chunk_sources[index])
-                chunks.append([raw[:, q * PACK : (q + 1) * PACK, :] for q in range(PASSES)])
+                h, position = divmod(index - FIRST_CHUNKS, STREAMS)
+                for q in range(PASSES):
+                    top = (SECOND_ORDER[position] * PASSES + q) * K_PASS
+                    nc.sync.dma_start(
+                        out=raw[:, :, q * HALF : (q + 1) * HALF],
+                        in_=Wk1[top : top + K_PASS, h * BANK : (h + 1) * BANK].rearrange("(j p) n -> p j n", p=P),
+                    )
+            chunks.append(raw)
 
         def regroup(index):
-            by_vector = grouped_pool.tile([P, HALF, PACK], BF16, align_bytes=64, bufs=2)
-            by_scalar = grouped_pool.tile([P, HALF, PACK], BF16, align_bytes=64)
+            grouped = grouped_pool.tile([P, C, PACK], BF16, align_bytes=64)
             nc.vector.tensor_copy(
-                out=by_vector[:].rearrange("p (c i) t -> p c t i", i=4),
-                in_=chunks[index][0].rearrange("p t (c i) -> p c t i", i=4),
+                out=grouped[:, 0:VECTOR_COLS, :].rearrange("p (c i) t -> p c t i", i=4),
+                in_=chunks[index][:, :, 0:VECTOR_COLS].rearrange("p t (c i) -> p c t i", i=4),
             )
             nc.scalar.copy(
-                out=by_scalar[:].rearrange("p (c i) t -> p c t i", i=4),
-                in_=chunks[index][1].rearrange("p t (c i) -> p c t i", i=4),
+                out=grouped[:, VECTOR_COLS:C, :].rearrange("p (c i) t -> p c t i", i=4),
+                in_=chunks[index][:, :, VECTOR_COLS:C].rearrange("p t (c i) -> p c t i", i=4),
             )
-            regrouped[index] = (by_vector, by_scalar)
+            regrouped[index] = grouped
             load_next_chunk()
 
         def quantise_chunk(index):
             for half in range(2):
+                cols = slice(half * HALF, (half + 1) * HALF)
                 if index < FIRST_CHUNKS:
                     weight, g = divmod(index, PASSES)
-                    cols = slice(half * HALF, (half + 1) * HALF)
                     words, scales = w1_words[weight][:, g, cols], w1_scales[weight][:, g, cols]
                 else:
                     h, position = divmod(index - FIRST_CHUNKS, STREAMS)
@@ -139,7 +137,7 @@ def tile_comformerconvedgelayer_pa_kernel(
                 nc.vector.quantize_mx(
                     out=words.bitcast(FP8X4),
                     scales=scales,
-                    in_=regrouped[index][half][:].rearrange("p c t -> p (c t)"),
+                    in_=regrouped[index][:, cols, :].rearrange("p c t -> p (c t)"),
                 )
 
         x_rows = {}
@@ -314,8 +312,8 @@ def tile_comformerconvedgelayer_pa_kernel(
 
         accs = open_banks()
         second_passes(FIRST_CHUNKS, accs)
-        for index in range(FIRST_CHUNKS + 2, len(chunk_sources) + 1):
-            if index < len(chunk_sources):
+        for index in range(FIRST_CHUNKS + 2, n_chunks + 1):
+            if index < n_chunks:
                 regroup(index)
             quantise_chunk(index - 1)
             if index - 1 == FIRST_CHUNKS + STREAMS:

@@ -227,9 +227,9 @@ def tile_comformerconvedgelayer_pa_kernel(
         def second_passes(index, accs):
             h, position = divmod(index - FIRST_CHUNKS, STREAMS)
             s = SECOND_ORDER[position]
-            for q in range(PASSES):
-                for b in range(E_BLOCKS):
-                    for t in range(T):
+            for b in range(E_BLOCKS):
+                for t in range(T):
+                    for q in range(PASSES):
                         unit = 0 if s == 0 else 1 + (s - 1) * T + t
                         e_cols = slice((q * E_BLOCKS + b) * P, (q * E_BLOCKS + b + 1) * P)
                         nc.tensor.matmul_mx(
@@ -254,7 +254,7 @@ def tile_comformerconvedgelayer_pa_kernel(
                         out=result[:], in0=accs[b * T + t][:], in1=bk1_all[:, n_cols], op=ADD
                     )
                     nc.scalar.activation(out=result[:], in_=result[:], func=SILU)
-                    nc.scalar.dma_start(out=out[b * P : (b + 1) * P, t, n_cols], in_=result[:])
+                    nc.sync.dma_start(out=out[b * P : (b + 1) * P, t, n_cols], in_=result[:])
 
         load_next_chunk()
         load_next_chunk()

from contextlib import ExitStack

import concourse.mybir as mybir
from concourse.masks import make_identity

F32 = mybir.dt.float32
BF16 = mybir.dt.bfloat16
U32 = mybir.dt.uint32
U8 = mybir.dt.uint8
FP8X4 = mybir.dt.float8_e4m3fn_x4
ADD = mybir.AluOpType.add
SILU = mybir.ActivationFunctionType.Silu

P = 128
PACK = 4
K_PASS = P * PACK
BANK = 512

E = 256
T = 3
C = 1024
E_BLOCKS = E // P
PASSES = C // K_PASS
STREAMS = 3
UNITS = 1 + T + T
HALF = BANK
VECTOR_COLS = 448
FIRST_WEIGHTS = 2 + T
FIRST_CHUNKS = FIRST_WEIGHTS * PASSES
SECOND_ORDER = (0, 2, 1)
RAW_BUFS = 4

FLOPS = 2 * 2 * UNITS * E * C * C


def tile_comformerconvedgelayer_pa_kernel(
    tc, edge, edge_nei_len, edge_nei_angle, Wk, bk, Wke, bke, We, Wk1, bk1, out
):
    nc = tc.nc
    m_tiles = C // P
    n_halves = C // BANK
    with ExitStack() as ctx:
        consts = ctx.enter_context(tc.tile_pool(name="consts", bufs=1))
        keep = ctx.enter_context(tc.tile_pool(name="keep", bufs=1))
        raw_pool = ctx.enter_context(tc.tile_pool(name="raw", bufs=RAW_BUFS))
        grouped_pool = ctx.enter_context(tc.tile_pool(name="grouped", bufs=3))
        first_w_pool = ctx.enter_context(tc.tile_pool(name="first_w", bufs=2))
        act_pool = ctx.enter_context(tc.tile_pool(name="act", bufs=4))
        result_pool = ctx.enter_context(tc.tile_pool(name="result", bufs=E_BLOCKS * T))
        psum = ctx.enter_context(tc.psum_pool(name="psum", bufs=8))

        bias_rows = consts.tile([P, P], BF16)
        nc.vector.memset(bias_rows[:], 0.0)
        nc.scalar.dma_start(out=bias_rows[0:m_tiles, :], in_=bk.rearrange("(m p) -> m p", p=P))
        nc.scalar.dma_start(
            out=bias_rows[m_tiles : (1 + T) * m_tiles, :],
            in_=bke.rearrange("t (m p) -> (t m) p", p=P),
        )
        bk1_row = consts.tile([P, C], BF16)
        nc.vector.memset(bk1_row[:], 0.0)
        nc.scalar.dma_start(out=bk1_row[0:1, :], in_=bk1.rearrange("(o c) -> o c", o=1))
        ones = consts.tile([P, P], BF16)
        nc.vector.memset(ones[:], 1.0)

        warm = consts.tile([P, 1], F32)
        nc.vector.memset(warm[:], 0.0)
        nc.scalar.activation(out=warm[:], in_=warm[:], func=SILU)

        ident_f32 = consts.tile([P, P], F32)
        make_identity(nc, ident_f32[:])
        ident_bf16 = consts.tile([P, P], BF16)
        make_identity(nc, ident_bf16[:])
        first_bias = consts.tile([P, (1 + T) * m_tiles], F32)
        bk1_all = consts.tile([P, C], F32)

        x_words = keep.tile([P, UNITS, PASSES * E], U32, align_bytes=64)
        x_scales = keep.tile([P, UNITS, PASSES * E], U8, align_bytes=64)
        h_words = keep.tile([P, UNITS, PASSES * E], U32, align_bytes=64)
        h_scales = keep.tile([P, UNITS, PASSES * E], U8, align_bytes=64)
        w2_words = keep.tile([P, n_halves, STREAMS * PASSES, BANK], U32, align_bytes=64)
        w2_scales = keep.tile([P, n_halves, STREAMS * PASSES, BANK], U8, align_bytes=64)
        we_words = keep.tile([P, PASSES, C], U32, align_bytes=64)
        we_scales = keep.tile([P, PASSES, C], U8, align_bytes=64)
        w1_words = {0: we_words}
        w1_scales = {0: we_scales}

        chunks = []
        regrouped = {}
        first_weights = (We, Wk, Wke[0], Wke[1], Wke[2])
        n_chunks = FIRST_CHUNKS + n_halves * STREAMS

        def load_next_chunk():
            index = len(chunks)
            if index == n_chunks:
                return
            raw = raw_pool.tile([P, PACK, C], BF16)
            if index < FIRST_CHUNKS:
                weight, g = divmod(index, PASSES)
                rows = first_weights[weight][g * K_PASS : (g + 1) * K_PASS, :]
                nc.sync.dma_start(
                    out=raw[:].rearrange("p (u e) c -> p u (e c)", u=2),
                    in_=rows.rearrange("(u p e) c -> p u (e c)", u=2, e=2),
                )
            else:
                h, position = divmod(index - FIRST_CHUNKS, STREAMS)
                for q in range(PASSES):
                    top = (SECOND_ORDER[position] * PASSES + q) * K_PASS
                    nc.sync.dma_start(
                        out=raw[:, :, q * HALF : (q + 1) * HALF],
                        in_=Wk1[top : top + K_PASS, h * BANK : (h + 1) * BANK].rearrange("(j p) n -> p j n", p=P),
                    )
            chunks.append(raw)

        def regroup(index):
            grouped = grouped_pool.tile([P, C, PACK], BF16, align_bytes=64)
            nc.vector.tensor_copy(
                out=grouped[:, 0:VECTOR_COLS, :].rearrange("p (c i) t -> p c t i", i=4),
                in_=chunks[index][:, :, 0:VECTOR_COLS].rearrange("p t (c i) -> p c t i", i=4),
            )
            nc.scalar.copy(
                out=grouped[:, VECTOR_COLS:C, :].rearrange("p (c i) t -> p c t i", i=4),
                in_=chunks[index][:, :, VECTOR_COLS:C].rearrange("p t (c i) -> p c t i", i=4),
            )
            regrouped[index] = grouped
            load_next_chunk()

        def quantise_chunk(index):
            for half in range(2):
                cols = slice(half * HALF, (half + 1) * HALF)
                if index < FIRST_CHUNKS:
                    weight, g = divmod(index, PASSES)
                    words, scales = w1_words[weight][:, g, cols], w1_scales[weight][:, g, cols]
                else:
                    h, position = divmod(index - FIRST_CHUNKS, STREAMS)
                    q = SECOND_ORDER[position] * PASSES + half
                    words, scales = w2_words[:, h, q, :], w2_scales[:, h, q, :]
                nc.vector.quantize_mx(
                    out=words.bitcast(FP8X4),
                    scales=scales,
                    in_=regrouped[index][:, cols, :].rearrange("p c t -> p (c t)"),
                )

        x_rows = {}
        x_grouped = {}

        def load_activations(unit):
            if unit == 0:
                source = edge
            elif unit <= T:
                source = edge_nei_len[:, unit - 1, :]
            else:
                source = edge_nei_angle[:, unit - 1 - T, :]
            x_rows[unit] = keep.tile([P, E_BLOCKS, C], BF16, name="x_rows%d" % unit)
            nc.sync.dma_start(out=x_rows[unit][:], in_=source.rearrange("(b p) k -> p b k", p=P))

        def transpose_activations(unit):
            grouped = act_pool.tile([P, PASSES * E * PACK], BF16, align_bytes=64, tag="x_grouped")
            grouped_pairs = grouped[:].bitcast(F32).rearrange("p (g r u) -> p g r u", g=PASSES, u=2)
            for b in range(E_BLOCKS):
                pairs = x_rows[unit][:, b, :].bitcast(F32)
                turned = psum.tile([P, BANK], F32, tag="bank")
                for w in range(BANK // P):
                    nc.tensor.transpose(
                        turned[:, w * P : (w + 1) * P], pairs[:, w * P : (w + 1) * P], ident_f32[:]
                    )
                nc.scalar.copy(
                    out=grouped_pairs[:, :, b * P : (b + 1) * P, :],
                    in_=turned[:].rearrange("p (g u r) -> p g r u", g=PASSES, u=2),
                )
            x_grouped[unit] = grouped

        def quantise_activations(unit):
            nc.vector.quantize_mx(
                out=x_words[:, unit, :].bitcast(FP8X4),
                scales=x_scales[:, unit, :],
                in_=x_grouped[unit][:],
            )

        first_accs = {}
        h_grouped = {}

        def first_passes(unit):
            weight = 1 + unit if unit <= T else 0
            words, scales = w1_words[weight], w1_scales[weight]
            first_accs[unit] = []
            for q in range(PASSES):
                for b in range(E_BLOCKS):
                    acc = psum.tile([P, BANK], F32, tag="bank")
                    for j in range(PACK):
                        m_cols = slice((q * PACK + j) * P, (q * PACK + j + 1) * P)
                        for g in range(PASSES):
                            e_cols = slice(g * E + b * P, g * E + (b + 1) * P)
                            nc.tensor.matmul_mx(
                                out=acc[:, j * P : (j + 1) * P],
                                lhsT=words[:, g, m_cols].bitcast(FP8X4),
                                lhsT_scale=scales[:, g, m_cols],
                                rhs=x_words[:, unit, e_cols].bitcast(FP8X4),
                                rhs_scale=x_scales[:, unit, e_cols],
                                start=(g == 0),
                                stop=(g == PASSES - 1),
                            )
                    first_accs[unit].append(acc)

        def first_out(unit):
            grouped = act_pool.tile([P, PASSES * E_BLOCKS, P, PACK], BF16, align_bytes=64, tag="h_grouped", bufs=3)
            for a, acc in enumerate(first_accs[unit]):
                interleaved = acc[:].rearrange("p (j r) -> p r j", j=PACK)
                if unit > T:
                    nc.scalar.copy(out=grouped[:, a], in_=interleaved)
                else:
                    first = unit * m_tiles + (a // E_BLOCKS) * PACK
                    nc.vector.tensor_tensor(
                        out=grouped[:, a],
                        in0=interleaved,
                        in1=first_bias[:, first : first + PACK].unsqueeze(1).to_broadcast([P, P, PACK]),
                        op=ADD,
                    )
            h_grouped[unit] = grouped

        def quantise_hidden(unit):
            nc.vector.quantize_mx(
                out=h_words[:, unit, :].bitcast(FP8X4),
                scales=h_scales[:, unit, :],
                in_=h_grouped[unit][:].rearrange("p a r j -> p (a r j)"),
            )

        def second_passes(index, accs):
            h, position = divmod(index - FIRST_CHUNKS, STREAMS)
            s = SECOND_ORDER[position]
            for b in range(E_BLOCKS):
                for t in range(T):
                    for q in range(PASSES):
                        unit = 0 if s == 0 else 1 + (s - 1) * T + t
                        e_cols = slice((q * E_BLOCKS + b) * P, (q * E_BLOCKS + b + 1) * P)
                        nc.tensor.matmul_mx(
                            out=accs[b * T + t][:],
                            lhsT=h_words[:, unit, e_cols].bitcast(FP8X4),
                            lhsT_scale=h_scales[:, unit, e_cols],
                            rhs=w2_words[:, h, s * PASSES + q, :].bitcast(FP8X4),
                            rhs_scale=w2_scales[:, h, s * PASSES + q, :],
                            start=(position == 0 and q == 0),
                            stop=(position == STREAMS - 1 and q == PASSES - 1),
                        )

        def open_banks():
            return [psum.tile([P, BANK], F32, tag="bank", name="acc2") for i in range(E_BLOCKS * T)]

        def finish(h, accs):
            n_cols = slice(h * BANK, (h + 1) * BANK)
            for b in range(E_BLOCKS):
                for t in range(T):
                    result = result_pool.tile([P, BANK], F32)
                    nc.vector.tensor_tensor(
                        out=result[:], in0=accs[b * T + t][:], in1=bk1_all[:, n_cols], op=ADD
                    )
                    nc.scalar.activation(out=result[:], in_=result[:], func=SILU)
                    nc.sync.dma_start(out=out[b * P : (b + 1) * P, t, n_cols], in_=result[:])

        load_next_chunk()
        load_next_chunk()
        for t in range(T):
            load_activations(1 + T + t)
        load_activations(0)
        load_next_chunk()

        for phase in range(FIRST_WEIGHTS + 1):
            arriving = phase - 1
            complete = phase - 2
            exy_out = T + phase - 1
            if 1 <= phase < FIRST_WEIGHTS:
                w1_words[phase] = first_w_pool.tile([P, PASSES, C], U32, align_bytes=64, name="w1_words")
                w1_scales[phase] = first_w_pool.tile([P, PASSES, C], U8, align_bytes=64, name="w1_scales")

            regroup(2 * phase)
            if phase < T:
                load_activations(1 + phase)
            if phase > 0:
                quantise_chunk(2 * phase - 1)
            if phase == 1:
                for t in range(T):
                    transpose_activations(1 + T + t)
                bias_cols = psum.tile([P, P], BF16, tag="bank")
                nc.tensor.transpose(bias_cols[:], bias_rows[:], ident_bf16[:])
                nc.vector.tensor_copy(out=first_bias[:], in_=bias_cols[:, 0 : (1 + T) * m_tiles])
            if 0 <= arriving <= T:
                transpose_activations(arriving)
            if complete >= 0:
                first_passes(complete)
            if 2 <= phase <= 1 + T:
                first_out(exy_out)

            regroup(2 * phase + 1)
            quantise_chunk(2 * phase)
            if phase == 1:
                for t in range(T):
                    quantise_activations(1 + T + t)
            if 0 <= arriving <= T:
                quantise_activations(arriving)
            if complete >= 0:
                first_out(complete)
                quantise_hidden(complete)
            if 2 <= phase <= 1 + T:
                quantise_hidden(exy_out)
            if 1 <= phase <= T:
                first_passes(T + phase)

        for h in range(n_halves):
            cols = slice(h * BANK, (h + 1) * BANK)
            spread = psum.tile([P, BANK], F32, tag="bank")
            nc.tensor.matmul(out=spread[:], lhsT=ones[:], rhs=bk1_row[:, cols], start=True, stop=True)
            nc.vector.tensor_copy(out=bk1_all[:, cols], in_=spread[:])

        accs = open_banks()
        second_passes(FIRST_CHUNKS, accs)
        for index in range(FIRST_CHUNKS + 2, n_chunks + 1):
            if index < n_chunks:
                regroup(index)
            quantise_chunk(index - 1)
            if index - 1 == FIRST_CHUNKS + STREAMS:
                finish(0, accs)
                accs = open_banks()
            second_passes(index - 1, accs)
        finish(1, accs)
